import numpy as np
import ml_dtypes


def mxq(x, axis, fmt="e4m3"):
    dtype, down = {"e4m3": (ml_dtypes.float8_e4m3fn, 7), "e5m2": (ml_dtypes.float8_e5m2, 14)}[fmt]
    v = np.moveaxis(np.asarray(x, np.float32).astype(ml_dtypes.bfloat16).astype(np.float64), axis, -1)
    blocks = v.reshape(v.shape[:-1] + (-1, 32))
    amax = np.abs(blocks).max(-1, keepdims=True)
    byte = np.maximum(np.where(amax > 0, np.frexp(amax)[1] - 1 + 127, 0) - down, 1)
    scale = np.exp2(byte - 127.0)
    codes = (blocks / scale).astype(np.float32).astype(dtype).astype(np.float64)
    return np.moveaxis((codes * scale).reshape(v.shape), -1, axis)


WIDE = False


def mx_kscale(k):
    if not WIDE:
        return np.ones(k)
    levels = np.array([20, -20, 10, -10, 0])
    a = np.random.permutation(np.resize(levels, k // 512 * 4)).reshape(k // 512, 4)
    idx = np.arange(k)
    return np.exp2(a[idx // 512, idx % 128 // 32])


BF16 = ml_dtypes.bfloat16


def bf(x):
    return np.asarray(x, np.float32).astype(BF16)


def f64(x):
    return np.asarray(x).astype(np.float64)


B, C, H, W, R = 2, 256, 32, 32, 4
N = H * W
NOISE = 0.5
GSCALE = 64.0


def mix(a, z):
    return sum(a[:, :, r, None] * z[:, r, None, :] for r in range(R))


def softmax(s):
    e = np.exp(s - s.max(-1, keepdims=True))
    return e / e.sum(-1, keepdims=True)


def setup_inputs():
    s = mx_kscale(N)
    z = np.random.standard_normal((B, R, N))
    a1 = np.random.standard_normal((B, C, R)) / np.sqrt(R)
    a2 = np.random.standard_normal((B, C, R)) / np.sqrt(R)
    x1 = mix(a1, z) + NOISE * np.random.standard_normal((B, C, N))
    x2 = mix(a2, z) + NOISE * np.random.standard_normal((B, C, N))
    u1 = a1 / np.sqrt((a1 * a1).sum(2, keepdims=True) + NOISE * NOISE)
    u2 = a2 / np.sqrt((a2 * a2).sum(2, keepdims=True) + NOISE * NOISE)
    logits1 = mix(u1 + u2, u1.transpose(0, 2, 1))
    logits2 = mix(u2 + u1, u2.transpose(0, 2, 1))
    x1 = x1 * s[None, None, :]
    g = np.random.standard_normal((B, N, C)) * np.exp2(np.random.randint(-12, 1, (B, N, 1))) * GSCALE / s[None, :, None]
    return {"logits1": bf(logits1), "logits2": bf(logits2),
            "x1": bf(x1.reshape(B, C, H, W)), "x2": bf(x2.reshape(B, C, H, W)),
            "grad_out": bf(g.reshape(B, C, H, W))}


def reference(logits1, logits2, x1, x2, grad_out):
    g = f64(grad_out).reshape(B, N, C)
    x = f64(x1).reshape(B, C, N)
    p = softmax(f64(logits1))
    gq = mxq(g, 1, "e5m2")
    xq = mxq(x, 2, "e4m3")
    d = gq.transpose(0, 2, 1) @ xq.transpose(0, 2, 1)
    return p * (d - (p * d).sum(-1, keepdims=True))

@@ -1,0 +1,181 @@
+from contextlib import ExitStack
+
+import concourse.masks as masks
+import concourse.mybir as mybir
+
+F32 = mybir.dt.float32
+BF16 = mybir.dt.bfloat16
+U32 = mybir.dt.uint32
+U8 = mybir.dt.uint8
+E4M3_X4 = mybir.dt.float8_e4m3fn_x4
+E5M2_X4 = mybir.dt.float8_e5m2_x4
+ALU = mybir.AluOpType
+ACT = mybir.ActivationFunctionType
+AXIS = mybir.AxisListType
+
+B = 2
+C = 256
+N_POS = 1024
+P = 128
+PACK = 4
+K_PASS = P * PACK
+PASSES = N_POS // K_PASS
+C_TILES = C // P
+ROW_TILES = B * C_TILES
+PAIR = 2
+HALVES = PACK // PAIR
+RUN = 4
+
+FLOPS = 2 * B * C * C * N_POS
+
+
+def tile_interfusion_pb_s_kernel(tc, logits1, logits2, x1, x2, grad_out, out):
+    nc = tc.nc
+
+    logit_rows = logits1.flatten_outer_dims().rearrange("(t p) k -> p t k", p=P)
+    x_rows = x1.rearrange("b k h w -> (b k) (h w)")
+    g_rows = grad_out.rearrange("b a h w -> (b a) (h w)")
+    out_rows = out.flatten_outer_dims()
+
+    with ExitStack() as ctx:
+        keep = ctx.enter_context(tc.tile_pool(name="keep", bufs=1))
+        psum = ctx.enter_context(tc.psum_pool(name="psum", bufs=1))
+
+        logit_sb = keep.tile([P, ROW_TILES, C], BF16)
+        nc.scalar.dma_start(out=logit_sb[:], in_=logit_rows)
+        x_sb = []
+        for r in range(ROW_TILES):
+            x_tile = keep.tile([P, N_POS], BF16, name="x_sb%d" % r)
+            nc.sync.dma_start(out=x_tile[:], in_=x_rows[r * P : (r + 1) * P, :])
+            x_sb.append(x_tile)
+        g_raw = []
+        for s in range(B * PASSES):
+            g_tile = keep.tile([P, PACK, C], BF16, name="g_raw%d" % s)
+            nc.sync.dma_start(
+                out=g_tile[:].rearrange("p j c -> p (j c)"), in_=g_rows[s * P : (s + 1) * P, :]
+            )
+            g_raw.append(g_tile)
+
+        ident = keep.tile([P, P], F32)
+        masks.make_identity(nc, ident[:])
+        warm_in = keep.tile([P, 1], F32)
+        warm_out = keep.tile([P, 1], F32)
+        nc.vector.memset(warm_in[:], 0.0)
+        nc.scalar.activation(out=warm_out[:], in_=warm_in[:], func=ACT.Exp)
+
+        row_max = keep.tile([P, ROW_TILES], F32)
+        neg_max = keep.tile([P, ROW_TILES], F32)
+        nc.vector.reduce_max(out=row_max[:], in_=logit_sb[:], axis=AXIS.X)
+        nc.vector.tensor_scalar_mul(out=neg_max[:], in0=row_max[:], scalar1=-1.0)
+
+        x_grouped = keep.tile([P, PASSES * B * C * PACK], BF16, align_bytes=64)
+        x_grouped_words = x_grouped[:].bitcast(F32).rearrange(
+            "p (g c u) -> p g c u", g=PASSES, u=HALVES
+        )
+        x_grouped_bf16 = x_grouped[:].rearrange("p (g e) -> p g e", g=PASSES)
+        x_codes = keep.tile([P, PASSES, B * C], U32, align_bytes=64)
+        x_scales = keep.tile([P, PASSES, B * C], U8, align_bytes=64)
+        exp_sb = keep.tile([P, ROW_TILES, C], F32)
+        row_sum = keep.tile([P, ROW_TILES], F32)
+        for r in range(ROW_TILES):
+            x_words = x_sb[r][:].bitcast(F32).rearrange(
+                "p (g i u) -> p g u i", g=PASSES, u=HALVES
+            )
+            x_t = psum.tile([P, PASSES, HALVES, P], F32, name="x_t%d" % r)
+            for g in range(PASSES):
+                for u in range(HALVES):
+                    nc.tensor.transpose(x_t[:, g, u, :], x_words[:, g, u, :], ident[:])
+            nc.scalar.copy(
+                out=x_grouped_words[:, :, r * P : (r + 1) * P, :],
+                in_=x_t[:].rearrange("p g u c -> p g c u"),
+            )
+            nc.scalar.activation(
+                out=exp_sb[:, r, :],
+                in_=logit_sb[:, r, :],
+                func=ACT.Exp,
+                bias=neg_max[:, r : r + 1],
+                scale=1.0,
+                accum_out=row_sum[:, r : r + 1],
+            )
+            if r % C_TILES == C_TILES - 1:
+                b = r // C_TILES
+                for g in range(PASSES):
+                    nc.vector.quantize_mx(
+                        out=x_codes[:, g, b * C : (b + 1) * C].bitcast(E4M3_X4),
+                        scales=x_scales[:, g, b * C : (b + 1) * C],
+                        in_=x_grouped_bf16[:, g, b * C * PACK : (b + 1) * C * PACK],
+                    )
+
+        inv_sum = keep.tile([P, ROW_TILES], F32)
+        neg_inv_sum = keep.tile([P, ROW_TILES], F32)
+        nc.vector.reciprocal(out=inv_sum[:], in_=row_sum[:])
+        nc.vector.tensor_scalar_mul(out=neg_inv_sum[:], in0=inv_sum[:], scalar1=-1.0)
+
+        d_ps = []
+        for t in range(ROW_TILES):
+            d_tile = psum.tile([P, B * C], F32, name="d_ps%d" % t)
+            d_ps.append(d_tile)
+        for s in range(B * PASSES):
+            b = s // PASSES
+            g = s % PASSES
+            g_grouped = keep.tile([P, C, PACK], BF16, name="g_grouped%d" % s, align_bytes=64)
+            for ct in range(C_TILES):
+                cols = slice(ct * P, (ct + 1) * P)
+                dst = g_grouped[:, cols, :].rearrange("p (c i) j -> p c j i", i=RUN)
+                src = g_raw[s][:, :, cols].rearrange("p j (c i) -> p c j i", i=RUN)
+                if ct == 0:
+                    nc.vector.tensor_copy(out=dst, in_=src)
+                else:
+                    nc.scalar.copy(out=dst, in_=src)
+            g_codes = keep.tile([P, C], U32, name="g_codes%d" % s, align_bytes=64)
+            g_scales = keep.tile([P, C], U8, name="g_scales%d" % s, align_bytes=64)
+            nc.vector.quantize_mx(
+                out=g_codes[:].bitcast(E5M2_X4),
+                scales=g_scales[:],
+                in_=g_grouped[:].rearrange("p c j -> p (c j)"),
+            )
+            for ct in range(C_TILES):
+                cols = slice(ct * P, (ct + 1) * P)
+                nc.tensor.matmul_mx(
+                    out=d_ps[b * C_TILES + ct][:],
+                    lhsT=g_codes[:, cols].bitcast(E5M2_X4),
+                    lhsT_scale=g_scales[:, cols],
+                    rhs=x_codes[:, g, :].bitcast(E4M3_X4),
+                    rhs_scale=x_scales[:, g, :],
+                    start=(g == 0),
+                    stop=(g == PASSES - 1),
+                )
+
+        pd_sum = keep.tile([P, ROW_TILES], F32)
+        neg_scale = keep.tile([P, ROW_TILES], F32)
+        for b in range(B):
+            tiles = slice(b * C_TILES, (b + 1) * C_TILES)
+            pd = []
+            for ct in range(C_TILES):
+                t = b * C_TILES + ct
+                pd_tile = keep.tile([P, C], F32, name="pd%d" % t)
+                nc.vector.scalar_tensor_tensor(
+                    out=pd_tile[:],
+                    in0=d_ps[t][:, b * C : (b + 1) * C],
+                    scalar=inv_sum[:, t : t + 1],
+                    in1=exp_sb[:, t, :],
+                    op0=ALU.mult,
+                    op1=ALU.mult,
+                    accum_out=pd_sum[:, t : t + 1],
+                )
+                pd.append(pd_tile)
+            nc.vector.tensor_mul(
+                out=neg_scale[:, tiles], in0=pd_sum[:, tiles], in1=neg_inv_sum[:, tiles]
+            )
+            for ct in range(C_TILES):
+                t = b * C_TILES + ct
+                result = keep.tile([P, C], F32, name="result%d" % t)
+                nc.vector.scalar_tensor_tensor(
+                    out=result[:],
+                    in0=exp_sb[:, t, :],
+                    scalar=neg_scale[:, t : t + 1],
+                    in1=pd[ct][:],
+                    op0=ALU.mult,
+                    op1=ALU.add,
+                )
+                nc.sync.dma_start(out=out_rows[t * P : (t + 1) * P, :], in_=result[:])

@@ -25,6 +25,8 @@ ROW_TILES = B * C_TILES
 PAIR = 2
 HALVES = PACK // PAIR
 RUN = 4
+PIECES = B * PASSES
+VECTOR_COLS = 64
 
 FLOPS = 2 * B * C * C * N_POS
 
@@ -40,34 +42,20 @@ def tile_interfusion_pb_s_kernel(tc, logits1, logits2, x1, x2, grad_out, out):
     with ExitStack() as ctx:
         keep = ctx.enter_context(tc.tile_pool(name="keep", bufs=1))
         psum = ctx.enter_context(tc.psum_pool(name="psum", bufs=1))
+        ctx.enter_context(tc.manual_schedule())
 
         logit_sb = keep.tile([P, ROW_TILES, C], BF16)
-        nc.scalar.dma_start(out=logit_sb[:], in_=logit_rows)
-        x_sb = []
-        for r in range(ROW_TILES):
-            x_tile = keep.tile([P, N_POS], BF16, name="x_sb%d" % r)
-            nc.sync.dma_start(out=x_tile[:], in_=x_rows[r * P : (r + 1) * P, :])
-            x_sb.append(x_tile)
-        g_raw = []
-        for s in range(B * PASSES):
-            g_tile = keep.tile([P, PACK, C], BF16, name="g_raw%d" % s)
-            nc.sync.dma_start(
-                out=g_tile[:].rearrange("p j c -> p (j c)"), in_=g_rows[s * P : (s + 1) * P, :]
-            )
-            g_raw.append(g_tile)
-
+        x_sb = [keep.tile([P, N_POS], BF16, name="x_sb%d" % r) for r in range(ROW_TILES)]
+        g_raw = [keep.tile([P, PACK, C], BF16, name="g_raw%d" % s) for s in range(PIECES)]
         ident = keep.tile([P, P], F32)
-        masks.make_identity(nc, ident[:])
         warm_in = keep.tile([P, 1], F32)
         warm_out = keep.tile([P, 1], F32)
-        nc.vector.memset(warm_in[:], 0.0)
-        nc.scalar.activation(out=warm_out[:], in_=warm_in[:], func=ACT.Exp)
-
         row_max = keep.tile([P, ROW_TILES], F32)
         neg_max = keep.tile([P, ROW_TILES], F32)
-        nc.vector.reduce_max(out=row_max[:], in_=logit_sb[:], axis=AXIS.X)
-        nc.vector.tensor_scalar_mul(out=neg_max[:], in0=row_max[:], scalar1=-1.0)
-
+        exp_sb = keep.tile([P, ROW_TILES, C], F32)
+        row_sum = keep.tile([P, ROW_TILES], F32)
+        inv_sum = keep.tile([P, ROW_TILES], F32)
+        neg_inv_sum = keep.tile([P, ROW_TILES], F32)
         x_grouped = keep.tile([P, PASSES * B * C * PACK], BF16, align_bytes=64)
         x_grouped_words = x_grouped[:].bitcast(F32).rearrange(
             "p (g c u) -> p g c u", g=PASSES, u=HALVES
@@ -75,107 +63,145 @@ def tile_interfusion_pb_s_kernel(tc, logits1, logits2, x1, x2, grad_out, out):
         x_grouped_bf16 = x_grouped[:].rearrange("p (g e) -> p g e", g=PASSES)
         x_codes = keep.tile([P, PASSES, B * C], U32, align_bytes=64)
         x_scales = keep.tile([P, PASSES, B * C], U8, align_bytes=64)
-        exp_sb = keep.tile([P, ROW_TILES, C], F32)
-        row_sum = keep.tile([P, ROW_TILES], F32)
-        for r in range(ROW_TILES):
-            x_words = x_sb[r][:].bitcast(F32).rearrange(
-                "p (g i u) -> p g u i", g=PASSES, u=HALVES
-            )
-            x_t = psum.tile([P, PASSES, HALVES, P], F32, name="x_t%d" % r)
+        x_t = [psum.tile([P, PASSES, HALVES, P], F32, name="x_t%d" % r) for r in range(ROW_TILES)]
+        g_grouped = [
+            keep.tile([P, C, PACK], BF16, name="g_grouped%d" % s, align_bytes=64)
+            for s in range(PIECES)
+        ]
+        g_codes = [keep.tile([P, C], U32, name="g_codes%d" % s, align_bytes=64) for s in range(PIECES)]
+        g_scales = [keep.tile([P, C], U8, name="g_scales%d" % s, align_bytes=64) for s in range(PIECES)]
+        d_ps = [psum.tile([P, B * C], F32, name="d_ps%d" % t) for t in range(ROW_TILES)]
+        pd = [keep.tile([P, C], F32, name="pd%d" % t) for t in range(ROW_TILES)]
+        pd_sum = keep.tile([P, ROW_TILES], F32)
+        neg_scale = keep.tile([P, ROW_TILES], F32)
+        result = [keep.tile([P, C], F32, name="result%d" % t) for t in range(ROW_TILES)]
+
+        def transpose_x(r):
+            x_words = x_sb[r][:].bitcast(F32).rearrange("p (g i u) -> p g u i", g=PASSES, u=HALVES)
             for g in range(PASSES):
                 for u in range(HALVES):
-                    nc.tensor.transpose(x_t[:, g, u, :], x_words[:, g, u, :], ident[:])
-            nc.scalar.copy(
-                out=x_grouped_words[:, :, r * P : (r + 1) * P, :],
-                in_=x_t[:].rearrange("p g u c -> p g c u"),
-            )
-            nc.scalar.activation(
-                out=exp_sb[:, r, :],
-                in_=logit_sb[:, r, :],
-                func=ACT.Exp,
-                bias=neg_max[:, r : r + 1],
-                scale=1.0,
-                accum_out=row_sum[:, r : r + 1],
-            )
-            if r % C_TILES == C_TILES - 1:
-                b = r // C_TILES
-                for g in range(PASSES):
-                    nc.vector.quantize_mx(
-                        out=x_codes[:, g, b * C : (b + 1) * C].bitcast(E4M3_X4),
-                        scales=x_scales[:, g, b * C : (b + 1) * C],
-                        in_=x_grouped_bf16[:, g, b * C * PACK : (b + 1) * C * PACK],
-                    )
+                    nc.tensor.transpose(x_t[r][:, g, u, :], x_words[:, g, u, :], ident[:])
 
-        inv_sum = keep.tile([P, ROW_TILES], F32)
-        neg_inv_sum = keep.tile([P, ROW_TILES], F32)
-        nc.vector.reciprocal(out=inv_sum[:], in_=row_sum[:])
-        nc.vector.tensor_scalar_mul(out=neg_inv_sum[:], in0=inv_sum[:], scalar1=-1.0)
+        def copy_out_x(r):
+            dst = x_grouped_words[:, :, r * P : (r + 1) * P, :]
+            src = x_t[r][:].rearrange("p g u c -> p g c u")
+            if r % 2 == 0:
+                nc.scalar.copy(out=dst, in_=src)
+            else:
+                nc.vector.tensor_copy(out=dst, in_=src)
 
-        d_ps = []
-        for t in range(ROW_TILES):
-            d_tile = psum.tile([P, B * C], F32, name="d_ps%d" % t)
-            d_ps.append(d_tile)
-        for s in range(B * PASSES):
+        def quantise_x(b):
+            for g in range(PASSES):
+                nc.vector.quantize_mx(
+                    out=x_codes[:, g, b * C : (b + 1) * C].bitcast(E4M3_X4),
+                    scales=x_scales[:, g, b * C : (b + 1) * C],
+                    in_=x_grouped_bf16[:, g, b * C * PACK : (b + 1) * C * PACK],
+                )
+
+        def softmax_exp(b):
+            for t in range(b * C_TILES, (b + 1) * C_TILES):
+                nc.scalar.activation(
+                    out=exp_sb[:, t, :],
+                    in_=logit_sb[:, t, :],
+                    func=ACT.Exp,
+                    bias=neg_max[:, t : t + 1],
+                    scale=1.0,
+                    accum_out=row_sum[:, t : t + 1],
+                )
+
+        def softmax_inverse(b):
+            tiles = slice(b * C_TILES, (b + 1) * C_TILES)
+            nc.vector.reciprocal(out=inv_sum[:, tiles], in_=row_sum[:, tiles])
+            nc.vector.tensor_scalar_mul(out=neg_inv_sum[:, tiles], in0=inv_sum[:, tiles], scalar1=-1.0)
+
+        def regroup_g(s):
+            for engine_copy, cols in (
+                (nc.vector.tensor_copy, slice(0, VECTOR_COLS)),
+                (nc.scalar.copy, slice(VECTOR_COLS, C)),
+            ):
+                engine_copy(
+                    out=g_grouped[s][:, cols, :].rearrange("p (c i) j -> p c j i", i=RUN),
+                    in_=g_raw[s][:, :, cols].rearrange("p j (c i) -> p c j i", i=RUN),
+                )
+
+        def quantise_g(s):
+            nc.vector.quantize_mx(
+                out=g_codes[s][:].bitcast(E5M2_X4),
+                scales=g_scales[s][:],
+                in_=g_grouped[s][:].rearrange("p c j -> p (c j)"),
+            )
+
+        def multiply(s):
             b = s // PASSES
             g = s % PASSES
-            g_grouped = keep.tile([P, C, PACK], BF16, name="g_grouped%d" % s, align_bytes=64)
-            for ct in range(C_TILES):
-                cols = slice(ct * P, (ct + 1) * P)
-                dst = g_grouped[:, cols, :].rearrange("p (c i) j -> p c j i", i=RUN)
-                src = g_raw[s][:, :, cols].rearrange("p j (c i) -> p c j i", i=RUN)
-                if ct == 0:
-                    nc.vector.tensor_copy(out=dst, in_=src)
-                else:
-                    nc.scalar.copy(out=dst, in_=src)
-            g_codes = keep.tile([P, C], U32, name="g_codes%d" % s, align_bytes=64)
-            g_scales = keep.tile([P, C], U8, name="g_scales%d" % s, align_bytes=64)
-            nc.vector.quantize_mx(
-                out=g_codes[:].bitcast(E5M2_X4),
-                scales=g_scales[:],
-                in_=g_grouped[:].rearrange("p c j -> p (c j)"),
-            )
             for ct in range(C_TILES):
                 cols = slice(ct * P, (ct + 1) * P)
                 nc.tensor.matmul_mx(
                     out=d_ps[b * C_TILES + ct][:],
-                    lhsT=g_codes[:, cols].bitcast(E5M2_X4),
-                    lhsT_scale=g_scales[:, cols],
+                    lhsT=g_codes[s][:, cols].bitcast(E5M2_X4),
+                    lhsT_scale=g_scales[s][:, cols],
                     rhs=x_codes[:, g, :].bitcast(E4M3_X4),
                     rhs_scale=x_scales[:, g, :],
                     start=(g == 0),
                     stop=(g == PASSES - 1),
                 )
 
-        pd_sum = keep.tile([P, ROW_TILES], F32)
-        neg_scale = keep.tile([P, ROW_TILES], F32)
-        for b in range(B):
-            tiles = slice(b * C_TILES, (b + 1) * C_TILES)
-            pd = []
-            for ct in range(C_TILES):
-                t = b * C_TILES + ct
-                pd_tile = keep.tile([P, C], F32, name="pd%d" % t)
-                nc.vector.scalar_tensor_tensor(
-                    out=pd_tile[:],
-                    in0=d_ps[t][:, b * C : (b + 1) * C],
-                    scalar=inv_sum[:, t : t + 1],
-                    in1=exp_sb[:, t, :],
-                    op0=ALU.mult,
-                    op1=ALU.mult,
-                    accum_out=pd_sum[:, t : t + 1],
-                )
-                pd.append(pd_tile)
-            nc.vector.tensor_mul(
-                out=neg_scale[:, tiles], in0=pd_sum[:, tiles], in1=neg_inv_sum[:, tiles]
+        def finish(t):
+            b = t // C_TILES
+            nc.vector.scalar_tensor_tensor(
+                out=pd[t][:],
+                in0=d_ps[t][:, b * C : (b + 1) * C],
+                scalar=inv_sum[:, t : t + 1],
+                in1=exp_sb[:, t, :],
+                op0=ALU.mult,
+                op1=ALU.mult,
+                accum_out=pd_sum[:, t : t + 1],
             )
-            for ct in range(C_TILES):
-                t = b * C_TILES + ct
-                result = keep.tile([P, C], F32, name="result%d" % t)
-                nc.vector.scalar_tensor_tensor(
-                    out=result[:],
-                    in0=exp_sb[:, t, :],
-                    scalar=neg_scale[:, t : t + 1],
-                    in1=pd[ct][:],
-                    op0=ALU.mult,
-                    op1=ALU.add,
-                )
-                nc.sync.dma_start(out=out_rows[t * P : (t + 1) * P, :], in_=result[:])
+            nc.vector.tensor_mul(
+                out=neg_scale[:, t : t + 1], in0=pd_sum[:, t : t + 1], in1=neg_inv_sum[:, t : t + 1]
+            )
+            nc.vector.scalar_tensor_tensor(
+                out=result[t][:],
+                in0=exp_sb[:, t, :],
+                scalar=neg_scale[:, t : t + 1],
+                in1=pd[t][:],
+                op0=ALU.mult,
+                op1=ALU.add,
+            )
+            nc.sync.dma_start(out=out_rows[t * P : (t + 1) * P, :], in_=result[t][:])
+
+        nc.scalar.dma_start(out=logit_sb[:], in_=logit_rows)
+        for r in range(ROW_TILES):
+            nc.sync.dma_start(out=x_sb[r][:], in_=x_rows[r * P : (r + 1) * P, :])
+        for s in range(PIECES):
+            nc.sync.dma_start(
+                out=g_raw[s][:].rearrange("p j c -> p (j c)"), in_=g_rows[s * P : (s + 1) * P, :]
+            )
+
+        masks.make_identity(nc, ident[:])
+        nc.vector.memset(warm_in[:], 0.0)
+        nc.scalar.activation(out=warm_out[:], in_=warm_in[:], func=ACT.Exp)
+        nc.vector.reduce_max(out=row_max[:], in_=logit_sb[:], axis=AXIS.X)
+        nc.vector.tensor_scalar_mul(out=neg_max[:], in0=row_max[:], scalar1=-1.0)
+
+        for b in range(B):
+            for r in range(b * C_TILES, (b + 1) * C_TILES):
+                transpose_x(r)
+                copy_out_x(r)
+            if b == 0:
+                softmax_exp(0)
+            quantise_x(b)
+        softmax_inverse(0)
+
+        regroup_g(0)
+        for s in range(PIECES):
+            if s + 1 < PIECES:
+                regroup_g(s + 1)
+            quantise_g(s)
+            multiply(s)
+            if s >= PASSES:
+                finish(s - PASSES)
+        softmax_exp(1)
+        softmax_inverse(1)
+        for t in range(PIECES - PASSES, ROW_TILES):
+            finish(t)

@@ -26,7 +26,6 @@ PAIR = 2
 HALVES = PACK // PAIR
 RUN = 4
 PIECES = B * PASSES
-VECTOR_COLS = 64
 
 FLOPS = 2 * B * C * C * N_POS
 
@@ -115,21 +114,23 @@ def tile_interfusion_pb_s_kernel(tc, logits1, logits2, x1, x2, grad_out, out):
             nc.vector.tensor_scalar_mul(out=neg_inv_sum[:, tiles], in0=inv_sum[:, tiles], scalar1=-1.0)
 
         def regroup_g(s):
-            for engine_copy, cols in (
-                (nc.vector.tensor_copy, slice(0, VECTOR_COLS)),
-                (nc.scalar.copy, slice(VECTOR_COLS, C)),
-            ):
-                engine_copy(
-                    out=g_grouped[s][:, cols, :].rearrange("p (c i) j -> p c j i", i=RUN),
-                    in_=g_raw[s][:, :, cols].rearrange("p j (c i) -> p c j i", i=RUN),
-                )
+            for ct in range(C_TILES):
+                cols = slice(ct * P, (ct + 1) * P)
+                dst = g_grouped[s][:, cols, :].rearrange("p (c i) j -> p c j i", i=RUN)
+                src = g_raw[s][:, :, cols].rearrange("p j (c i) -> p c j i", i=RUN)
+                if ct == 0:
+                    nc.vector.tensor_copy(out=dst, in_=src)
+                else:
+                    nc.scalar.copy(out=dst, in_=src)
 
         def quantise_g(s):
-            nc.vector.quantize_mx(
-                out=g_codes[s][:].bitcast(E5M2_X4),
-                scales=g_scales[s][:],
-                in_=g_grouped[s][:].rearrange("p c j -> p (c j)"),
-            )
+            for ct in range(C_TILES):
+                cols = slice(ct * P, (ct + 1) * P)
+                nc.vector.quantize_mx(
+                    out=g_codes[s][:, cols].bitcast(E5M2_X4),
+                    scales=g_scales[s][:, cols],
+                    in_=g_grouped[s][:, cols, :].rearrange("p c j -> p (c j)"),
+                )
 
         def multiply(s):
             b = s // PASSES
@@ -146,31 +147,33 @@ def tile_interfusion_pb_s_kernel(tc, logits1, logits2, x1, x2, grad_out, out):
                     stop=(g == PASSES - 1),
                 )
 
-        def finish(t):
-            b = t // C_TILES
-            nc.vector.scalar_tensor_tensor(
-                out=pd[t][:],
-                in0=d_ps[t][:, b * C : (b + 1) * C],
-                scalar=inv_sum[:, t : t + 1],
-                in1=exp_sb[:, t, :],
-                op0=ALU.mult,
-                op1=ALU.mult,
-                accum_out=pd_sum[:, t : t + 1],
-            )
+        def finish(b):
+            tiles = slice(b * C_TILES, (b + 1) * C_TILES)
+            for t in range(b * C_TILES, (b + 1) * C_TILES):
+                nc.vector.scalar_tensor_tensor(
+                    out=pd[t][:],
+                    in0=d_ps[t][:, b * C : (b + 1) * C],
+                    scalar=inv_sum[:, t : t + 1],
+                    in1=exp_sb[:, t, :],
+                    op0=ALU.mult,
+                    op1=ALU.mult,
+                    accum_out=pd_sum[:, t : t + 1],
+                )
             nc.vector.tensor_mul(
-                out=neg_scale[:, t : t + 1], in0=pd_sum[:, t : t + 1], in1=neg_inv_sum[:, t : t + 1]
+                out=neg_scale[:, tiles], in0=pd_sum[:, tiles], in1=neg_inv_sum[:, tiles]
             )
-            nc.vector.scalar_tensor_tensor(
-                out=result[t][:],
-                in0=exp_sb[:, t, :],
-                scalar=neg_scale[:, t : t + 1],
-                in1=pd[t][:],
-                op0=ALU.mult,
-                op1=ALU.add,
-            )
-            nc.sync.dma_start(out=out_rows[t * P : (t + 1) * P, :], in_=result[t][:])
+            for t in range(b * C_TILES, (b + 1) * C_TILES):
+                nc.vector.scalar_tensor_tensor(
+                    out=result[t][:],
+                    in0=exp_sb[:, t, :],
+                    scalar=neg_scale[:, t : t + 1],
+                    in1=pd[t][:],
+                    op0=ALU.mult,
+                    op1=ALU.add,
+                )
+                nc.sync.dma_start(out=out_rows[t * P : (t + 1) * P, :], in_=result[t][:])
 
-        nc.scalar.dma_start(out=logit_sb[:], in_=logit_rows)
+        nc.sync.dma_start(out=logit_sb[:], in_=logit_rows)
         for r in range(ROW_TILES):
             nc.sync.dma_start(out=x_sb[r][:], in_=x_rows[r * P : (r + 1) * P, :])
         for s in range(PIECES):
@@ -199,9 +202,8 @@ def tile_interfusion_pb_s_kernel(tc, logits1, logits2, x1, x2, grad_out, out):
                 regroup_g(s + 1)
             quantise_g(s)
             multiply(s)
-            if s >= PASSES:
-                finish(s - PASSES)
         softmax_exp(1)
+
+        finish(0)
         softmax_inverse(1)
-        for t in range(PIECES - PASSES, ROW_TILES):
-            finish(t)
+        finish(1)

@@ -54,7 +54,7 @@ def tile_interfusion_pb_s_kernel(tc, logits1, logits2, x1, x2, grad_out, out):
         exp_sb = keep.tile([P, ROW_TILES, C], F32)
         row_sum = keep.tile([P, ROW_TILES], F32)
         inv_sum = keep.tile([P, ROW_TILES], F32)
-        neg_inv_sum = keep.tile([P, ROW_TILES], F32)
+        neg_inv_sq = keep.tile([P, ROW_TILES], F32)
         x_grouped = keep.tile([P, PASSES * B * C * PACK], BF16, align_bytes=64)
         x_grouped_words = x_grouped[:].bitcast(F32).rearrange(
             "p (g c u) -> p g c u", g=PASSES, u=HALVES
@@ -70,9 +70,9 @@ def tile_interfusion_pb_s_kernel(tc, logits1, logits2, x1, x2, grad_out, out):
         g_codes = [keep.tile([P, C], U32, name="g_codes%d" % s, align_bytes=64) for s in range(PIECES)]
         g_scales = [keep.tile([P, C], U8, name="g_scales%d" % s, align_bytes=64) for s in range(PIECES)]
         d_ps = [psum.tile([P, B * C], F32, name="d_ps%d" % t) for t in range(ROW_TILES)]
-        pd = [keep.tile([P, C], F32, name="pd%d" % t) for t in range(ROW_TILES)]
-        pd_sum = keep.tile([P, ROW_TILES], F32)
-        neg_scale = keep.tile([P, ROW_TILES], F32)
+        unread = [keep.tile([P, C], F32, name="unread%d" % t) for t in range(ROW_TILES)]
+        shift = keep.tile([P, ROW_TILES], F32)
+        centred = [keep.tile([P, C], F32, name="centred%d" % t) for t in range(ROW_TILES)]
         result = [keep.tile([P, C], F32, name="result%d" % t) for t in range(ROW_TILES)]
 
         def transpose_x(r):
@@ -111,7 +111,14 @@ def tile_interfusion_pb_s_kernel(tc, logits1, logits2, x1, x2, grad_out, out):
         def softmax_inverse(b):
             tiles = slice(b * C_TILES, (b + 1) * C_TILES)
             nc.vector.reciprocal(out=inv_sum[:, tiles], in_=row_sum[:, tiles])
-            nc.vector.tensor_scalar_mul(out=neg_inv_sum[:, tiles], in0=inv_sum[:, tiles], scalar1=-1.0)
+            nc.vector.scalar_tensor_tensor(
+                out=neg_inv_sq[:, tiles],
+                in0=inv_sum[:, tiles],
+                scalar=-1.0,
+                in1=inv_sum[:, tiles],
+                op0=ALU.mult,
+                op1=ALU.mult,
+            )
 
         def regroup_g(s):
             for ct in range(C_TILES):
@@ -147,31 +154,32 @@ def tile_interfusion_pb_s_kernel(tc, logits1, logits2, x1, x2, grad_out, out):
                     stop=(g == PASSES - 1),
                 )
 
-        def finish(b):
-            tiles = slice(b * C_TILES, (b + 1) * C_TILES)
-            for t in range(b * C_TILES, (b + 1) * C_TILES):
-                nc.vector.scalar_tensor_tensor(
-                    out=pd[t][:],
-                    in0=d_ps[t][:, b * C : (b + 1) * C],
-                    scalar=inv_sum[:, t : t + 1],
-                    in1=exp_sb[:, t, :],
-                    op0=ALU.mult,
-                    op1=ALU.mult,
-                    accum_out=pd_sum[:, t : t + 1],
-                )
-            nc.vector.tensor_mul(
-                out=neg_scale[:, tiles], in0=pd_sum[:, tiles], in1=neg_inv_sum[:, tiles]
+        def weighted_sum(t):
+            b = t // C_TILES
+            nc.vector.scalar_tensor_tensor(
+                out=unread[t][:],
+                in0=d_ps[t][:, b * C : (b + 1) * C],
+                scalar=neg_inv_sq[:, t : t + 1],
+                in1=exp_sb[:, t, :],
+                op0=ALU.mult,
+                op1=ALU.mult,
+                accum_out=shift[:, t : t + 1],
             )
-            for t in range(b * C_TILES, (b + 1) * C_TILES):
-                nc.vector.scalar_tensor_tensor(
-                    out=result[t][:],
-                    in0=exp_sb[:, t, :],
-                    scalar=neg_scale[:, t : t + 1],
-                    in1=pd[t][:],
-                    op0=ALU.mult,
-                    op1=ALU.add,
-                )
-                nc.sync.dma_start(out=out_rows[t * P : (t + 1) * P, :], in_=result[t][:])
+
+        def centre(t):
+            b = t // C_TILES
+            nc.scalar.activation(
+                out=centred[t][:],
+                in_=d_ps[t][:, b * C : (b + 1) * C],
+                func=ACT.Identity,
+                bias=shift[:, t : t + 1],
+                scale=inv_sum[:, t : t + 1],
+            )
+
+        def product(t):
+            engine = nc.gpsimd if t // C_TILES == 0 else nc.vector
+            engine.tensor_tensor(out=result[t][:], in0=centred[t][:], in1=exp_sb[:, t, :], op=ALU.mult)
+            nc.sync.dma_start(out=out_rows[t * P : (t + 1) * P, :], in_=result[t][:])
 
         nc.sync.dma_start(out=logit_sb[:], in_=logit_rows)
         for r in range(ROW_TILES):
@@ -204,6 +212,11 @@ def tile_interfusion_pb_s_kernel(tc, logits1, logits2, x1, x2, grad_out, out):
             multiply(s)
         softmax_exp(1)
 
-        finish(0)
-        softmax_inverse(1)
-        finish(1)
+        for b in range(B):
+            if b > 0:
+                softmax_inverse(b)
+            for t in range(b * C_TILES, (b + 1) * C_TILES):
+                weighted_sum(t)
+            for t in range(b * C_TILES, (b + 1) * C_TILES):
+                centre(t)
+                product(t)

@@ -5,6 +5,7 @@ import concourse.mybir as mybir
 
 F32 = mybir.dt.float32
 BF16 = mybir.dt.bfloat16
+I32 = mybir.dt.int32
 U32 = mybir.dt.uint32
 U8 = mybir.dt.uint8
 E4M3_X4 = mybir.dt.float8_e4m3fn_x4
@@ -26,6 +27,7 @@ PAIR = 2
 HALVES = PACK // PAIR
 RUN = 4
 PIECES = B * PASSES
+N_MOVING = 2 * C
 
 FLOPS = 2 * B * C * C * N_POS
 
@@ -55,13 +57,12 @@ def tile_interfusion_pb_s_kernel(tc, logits1, logits2, x1, x2, grad_out, out):
         row_sum = keep.tile([P, ROW_TILES], F32)
         inv_sum = keep.tile([P, ROW_TILES], F32)
         neg_inv_sq = keep.tile([P, ROW_TILES], F32)
-        x_grouped = keep.tile([P, PASSES * B * C * PACK], BF16, align_bytes=64)
+        x_grouped = keep.tile([P, B * PASSES * C * PACK], BF16, align_bytes=64)
         x_grouped_words = x_grouped[:].bitcast(F32).rearrange(
-            "p (g c u) -> p g c u", g=PASSES, u=HALVES
+            "p (b g c u) -> p b g c u", b=B, g=PASSES, u=HALVES
         )
-        x_grouped_bf16 = x_grouped[:].rearrange("p (g e) -> p g e", g=PASSES)
-        x_codes = keep.tile([P, PASSES, B * C], U32, align_bytes=64)
-        x_scales = keep.tile([P, PASSES, B * C], U8, align_bytes=64)
+        x_codes = keep.tile([P, (1 + B * PASSES) * C], U32, align_bytes=64)
+        x_scales = keep.tile([P, (1 + B * PASSES) * C], U8, align_bytes=64)
         x_t = [psum.tile([P, PASSES, HALVES, P], F32, name="x_t%d" % r) for r in range(ROW_TILES)]
         g_grouped = [
             keep.tile([P, C, PACK], BF16, name="g_grouped%d" % s, align_bytes=64)
@@ -69,11 +70,19 @@ def tile_interfusion_pb_s_kernel(tc, logits1, logits2, x1, x2, grad_out, out):
         ]
         g_codes = [keep.tile([P, C], U32, name="g_codes%d" % s, align_bytes=64) for s in range(PIECES)]
         g_scales = [keep.tile([P, C], U8, name="g_scales%d" % s, align_bytes=64) for s in range(PIECES)]
-        d_ps = [psum.tile([P, B * C], F32, name="d_ps%d" % t) for t in range(ROW_TILES)]
+        d_ps = [psum.tile([P, N_MOVING], F32, name="d_ps%d" % t) for t in range(ROW_TILES)]
         unread = [keep.tile([P, C], F32, name="unread%d" % t) for t in range(ROW_TILES)]
         shift = keep.tile([P, ROW_TILES], F32)
         centred = [keep.tile([P, C], F32, name="centred%d" % t) for t in range(ROW_TILES)]
         result = [keep.tile([P, C], F32, name="result%d" % t) for t in range(ROW_TILES)]
+
+        def load_x(r):
+            nc.sync.dma_start(out=x_sb[r][:], in_=x_rows[r * P : (r + 1) * P, :])
+
+        def load_g(s):
+            nc.sync.dma_start(
+                out=g_raw[s][:].rearrange("p j c -> p (j c)"), in_=g_rows[s * P : (s + 1) * P, :]
+            )
 
         def transpose_x(r):
             x_words = x_sb[r][:].bitcast(F32).rearrange("p (g i u) -> p g u i", g=PASSES, u=HALVES)
@@ -82,31 +91,30 @@ def tile_interfusion_pb_s_kernel(tc, logits1, logits2, x1, x2, grad_out, out):
                     nc.tensor.transpose(x_t[r][:, g, u, :], x_words[:, g, u, :], ident[:])
 
         def copy_out_x(r):
-            dst = x_grouped_words[:, :, r * P : (r + 1) * P, :]
+            b = r // C_TILES
+            h = r % C_TILES
+            dst = x_grouped_words[:, b, :, h * P : (h + 1) * P, :]
             src = x_t[r][:].rearrange("p g u c -> p g c u")
-            if r % 2 == 0:
-                nc.scalar.copy(out=dst, in_=src)
-            else:
-                nc.vector.tensor_copy(out=dst, in_=src)
+            nc.scalar.copy(out=dst, in_=src)
 
         def quantise_x(b):
-            for g in range(PASSES):
-                nc.vector.quantize_mx(
-                    out=x_codes[:, g, b * C : (b + 1) * C].bitcast(E4M3_X4),
-                    scales=x_scales[:, g, b * C : (b + 1) * C],
-                    in_=x_grouped_bf16[:, g, b * C * PACK : (b + 1) * C * PACK],
-                )
+            first = (1 + b * PASSES) * C
+            width = PASSES * C
+            nc.vector.quantize_mx(
+                out=x_codes[:, first : first + width].bitcast(E4M3_X4),
+                scales=x_scales[:, first : first + width],
+                in_=x_grouped[:, b * width * PACK : (b + 1) * width * PACK],
+            )
 
-        def softmax_exp(b):
-            for t in range(b * C_TILES, (b + 1) * C_TILES):
-                nc.scalar.activation(
-                    out=exp_sb[:, t, :],
-                    in_=logit_sb[:, t, :],
-                    func=ACT.Exp,
-                    bias=neg_max[:, t : t + 1],
-                    scale=1.0,
-                    accum_out=row_sum[:, t : t + 1],
-                )
+        def softmax_exp(t):
+            nc.scalar.activation(
+                out=exp_sb[:, t, :],
+                in_=logit_sb[:, t, :],
+                func=ACT.Exp,
+                bias=neg_max[:, t : t + 1],
+                scale=1.0,
+                accum_out=row_sum[:, t : t + 1],
+            )
 
         def softmax_inverse(b):
             tiles = slice(b * C_TILES, (b + 1) * C_TILES)
@@ -120,45 +128,42 @@ def tile_interfusion_pb_s_kernel(tc, logits1, logits2, x1, x2, grad_out, out):
                 op1=ALU.mult,
             )
 
-        def regroup_g(s):
-            for ct in range(C_TILES):
-                cols = slice(ct * P, (ct + 1) * P)
-                dst = g_grouped[s][:, cols, :].rearrange("p (c i) j -> p c j i", i=RUN)
-                src = g_raw[s][:, :, cols].rearrange("p j (c i) -> p c j i", i=RUN)
-                if ct == 0:
-                    nc.vector.tensor_copy(out=dst, in_=src)
-                else:
-                    nc.scalar.copy(out=dst, in_=src)
+        def regroup_g(s, ct, engine):
+            cols = slice(ct * P, (ct + 1) * P)
+            dst = g_grouped[s][:, cols, :].rearrange("p (c i) j -> p c j i", i=RUN)
+            src = g_raw[s][:, :, cols].rearrange("p j (c i) -> p c j i", i=RUN)
+            if engine == "vector":
+                nc.vector.tensor_copy(out=dst, in_=src)
+            else:
+                nc.scalar.copy(out=dst, in_=src)
 
-        def quantise_g(s):
-            for ct in range(C_TILES):
-                cols = slice(ct * P, (ct + 1) * P)
-                nc.vector.quantize_mx(
-                    out=g_codes[s][:, cols].bitcast(E5M2_X4),
-                    scales=g_scales[s][:, cols],
-                    in_=g_grouped[s][:, cols, :].rearrange("p c j -> p (c j)"),
-                )
+        def quantise_g(s, ct):
+            cols = slice(ct * P, (ct + 1) * P)
+            nc.vector.quantize_mx(
+                out=g_codes[s][:, cols].bitcast(E5M2_X4),
+                scales=g_scales[s][:, cols],
+                in_=g_grouped[s][:, cols, :].rearrange("p c j -> p (c j)"),
+            )
 
-        def multiply(s):
+        def multiply(s, ct):
             b = s // PASSES
             g = s % PASSES
-            for ct in range(C_TILES):
-                cols = slice(ct * P, (ct + 1) * P)
-                nc.tensor.matmul_mx(
-                    out=d_ps[b * C_TILES + ct][:],
-                    lhsT=g_codes[s][:, cols].bitcast(E5M2_X4),
-                    lhsT_scale=g_scales[s][:, cols],
-                    rhs=x_codes[:, g, :].bitcast(E4M3_X4),
-                    rhs_scale=x_scales[:, g, :],
-                    start=(g == 0),
-                    stop=(g == PASSES - 1),
-                )
+            cols = slice(ct * P, (ct + 1) * P)
+            first = (b * PASSES + g) * C
+            nc.tensor.matmul_mx(
+                out=d_ps[b * C_TILES + ct][:],
+                lhsT=g_codes[s][:, cols].bitcast(E5M2_X4),
+                lhsT_scale=g_scales[s][:, cols],
+                rhs=x_codes[:, first : first + N_MOVING].bitcast(E4M3_X4),
+                rhs_scale=x_scales[:, first : first + N_MOVING],
+                start=(g == 0),
+                stop=(g == PASSES - 1),
+            )
 
         def weighted_sum(t):
-            b = t // C_TILES
             nc.vector.scalar_tensor_tensor(
                 out=unread[t][:],
-                in0=d_ps[t][:, b * C : (b + 1) * C],
+                in0=d_ps[t][:, C:N_MOVING],
                 scalar=neg_inv_sq[:, t : t + 1],
                 in1=exp_sb[:, t, :],
                 op0=ALU.mult,
@@ -167,10 +172,9 @@ def tile_interfusion_pb_s_kernel(tc, logits1, logits2, x1, x2, grad_out, out):
             )
 
         def centre(t):
-            b = t // C_TILES
             nc.scalar.activation(
                 out=centred[t][:],
-                in_=d_ps[t][:, b * C : (b + 1) * C],
+                in_=d_ps[t][:, C:N_MOVING],
                 func=ACT.Identity,
                 bias=shift[:, t : t + 1],
                 scale=inv_sum[:, t : t + 1],
@@ -181,40 +185,63 @@ def tile_interfusion_pb_s_kernel(tc, logits1, logits2, x1, x2, grad_out, out):
             engine.tensor_tensor(out=result[t][:], in0=centred[t][:], in1=exp_sb[:, t, :], op=ALU.mult)
             nc.sync.dma_start(out=out_rows[t * P : (t + 1) * P, :], in_=result[t][:])
 
+        load_g(0)
+        load_x(0)
         nc.sync.dma_start(out=logit_sb[:], in_=logit_rows)
-        for r in range(ROW_TILES):
-            nc.sync.dma_start(out=x_sb[r][:], in_=x_rows[r * P : (r + 1) * P, :])
-        for s in range(PIECES):
-            nc.sync.dma_start(
-                out=g_raw[s][:].rearrange("p j c -> p (j c)"), in_=g_rows[s * P : (s + 1) * P, :]
-            )
+        load_x(1)
+        load_g(1)
+        load_x(2)
+        load_g(2)
+        load_x(3)
+        load_g(3)
 
         masks.make_identity(nc, ident[:])
         nc.vector.memset(warm_in[:], 0.0)
         nc.scalar.activation(out=warm_out[:], in_=warm_in[:], func=ACT.Exp)
+        nc.vector.memset(x_codes[:, 0:C].bitcast(I32), 0)
+        nc.vector.memset(x_scales[:, 0:C].bitcast(I32), 0)
+
+        regroup_g(0, 0, "vector")
+        regroup_g(0, 1, "scalar")
+        quantise_g(0, 0)
+        quantise_g(0, 1)
+        transpose_x(0)
+        copy_out_x(0)
         nc.vector.reduce_max(out=row_max[:], in_=logit_sb[:], axis=AXIS.X)
         nc.vector.tensor_scalar_mul(out=neg_max[:], in0=row_max[:], scalar1=-1.0)
-
-        for b in range(B):
-            for r in range(b * C_TILES, (b + 1) * C_TILES):
-                transpose_x(r)
-                copy_out_x(r)
-            if b == 0:
-                softmax_exp(0)
-            quantise_x(b)
-        softmax_inverse(0)
-
-        regroup_g(0)
-        for s in range(PIECES):
-            if s + 1 < PIECES:
-                regroup_g(s + 1)
-            quantise_g(s)
-            multiply(s)
+        transpose_x(1)
+        regroup_g(1, 0, "vector")
+        regroup_g(1, 1, "scalar")
+        copy_out_x(1)
+        quantise_g(1, 0)
+        quantise_g(1, 1)
+        transpose_x(2)
+        regroup_g(2, 0, "vector")
+        regroup_g(2, 1, "scalar")
+        quantise_x(0)
+        copy_out_x(2)
+        quantise_g(2, 0)
+        softmax_exp(0)
+        transpose_x(3)
+        regroup_g(3, 0, "vector")
+        regroup_g(3, 1, "vector")
+        quantise_g(3, 0)
+        quantise_g(3, 1)
+        copy_out_x(3)
+        quantise_g(2, 1)
+        quantise_x(1)
+        for s in range(PASSES):
+            for ct in range(C_TILES):
+                multiply(s, ct)
         softmax_exp(1)
+        softmax_exp(2)
+        softmax_exp(3)
+        for ct in range(C_TILES):
+            for s in range(PASSES, PIECES):
+                multiply(s, ct)
 
         for b in range(B):
-            if b > 0:
-                softmax_inverse(b)
+            softmax_inverse(b)
             for t in range(b * C_TILES, (b + 1) * C_TILES):
                 weighted_sum(t)
             for t in range(b * C_TILES, (b + 1) * C_TILES):

@@ -51,12 +51,12 @@ def tile_interfusion_pb_s_kernel(tc, logits1, logits2, x1, x2, grad_out, out):
         ident = keep.tile([P, P], F32)
         warm_in = keep.tile([P, 1], F32)
         warm_out = keep.tile([P, 1], F32)
-        row_max = keep.tile([P, ROW_TILES], F32)
         neg_max = keep.tile([P, ROW_TILES], F32)
         exp_sb = keep.tile([P, ROW_TILES, C], F32)
         row_sum = keep.tile([P, ROW_TILES], F32)
         inv_sum = keep.tile([P, ROW_TILES], F32)
-        neg_inv_sq = keep.tile([P, ROW_TILES], F32)
+        inv_sq = keep.tile([P, C_TILES], F32)
+        prob_sb = keep.tile([P, C_TILES, C], F32)
         x_grouped = keep.tile([P, B * PASSES * C * PACK], BF16, align_bytes=64)
         x_grouped_words = x_grouped[:].bitcast(F32).rearrange(
             "p (b g c u) -> p b g c u", b=B, g=PASSES, u=HALVES
@@ -72,7 +72,8 @@ def tile_interfusion_pb_s_kernel(tc, logits1, logits2, x1, x2, grad_out, out):
         g_scales = [keep.tile([P, C], U8, name="g_scales%d" % s, align_bytes=64) for s in range(PIECES)]
         d_ps = [psum.tile([P, N_MOVING], F32, name="d_ps%d" % t) for t in range(ROW_TILES)]
         unread = [keep.tile([P, C], F32, name="unread%d" % t) for t in range(ROW_TILES)]
-        shift = keep.tile([P, ROW_TILES], F32)
+        dot = keep.tile([P, ROW_TILES], F32)
+        shift = keep.tile([P, C_TILES], F32)
         centred = [keep.tile([P, C], F32, name="centred%d" % t) for t in range(ROW_TILES)]
         result = [keep.tile([P, C], F32, name="result%d" % t) for t in range(ROW_TILES)]
 
@@ -119,13 +120,18 @@ def tile_interfusion_pb_s_kernel(tc, logits1, logits2, x1, x2, grad_out, out):
         def softmax_inverse(b):
             tiles = slice(b * C_TILES, (b + 1) * C_TILES)
             nc.vector.reciprocal(out=inv_sum[:, tiles], in_=row_sum[:, tiles])
-            nc.vector.scalar_tensor_tensor(
-                out=neg_inv_sq[:, tiles],
-                in0=inv_sum[:, tiles],
-                scalar=-1.0,
-                in1=inv_sum[:, tiles],
-                op0=ALU.mult,
-                op1=ALU.mult,
+
+        def softmax_inverse_squared():
+            nc.vector.tensor_tensor(
+                out=inv_sq[:], in0=inv_sum[:, 0:C_TILES], in1=inv_sum[:, 0:C_TILES], op=ALU.mult
+            )
+
+        def probabilities(t):
+            nc.scalar.activation(
+                out=prob_sb[:, t - C_TILES, :],
+                in_=exp_sb[:, t, :],
+                func=ACT.Copy,
+                scale=inv_sum[:, t : t + 1],
             )
 
         def regroup_g(s, ct, engine):
@@ -137,12 +143,11 @@ def tile_interfusion_pb_s_kernel(tc, logits1, logits2, x1, x2, grad_out, out):
             else:
                 nc.scalar.copy(out=dst, in_=src)
 
-        def quantise_g(s, ct):
-            cols = slice(ct * P, (ct + 1) * P)
+        def quantise_g(s):
             nc.vector.quantize_mx(
-                out=g_codes[s][:, cols].bitcast(E5M2_X4),
-                scales=g_scales[s][:, cols],
-                in_=g_grouped[s][:, cols, :].rearrange("p c j -> p (c j)"),
+                out=g_codes[s][:].bitcast(E5M2_X4),
+                scales=g_scales[s][:],
+                in_=g_grouped[s][:].rearrange("p c j -> p (c j)"),
             )
 
         def multiply(s, ct):
@@ -164,14 +169,17 @@ def tile_interfusion_pb_s_kernel(tc, logits1, logits2, x1, x2, grad_out, out):
             nc.vector.scalar_tensor_tensor(
                 out=unread[t][:],
                 in0=d_ps[t][:, C:N_MOVING],
-                scalar=neg_inv_sq[:, t : t + 1],
+                scalar=-1.0 if t < C_TILES else inv_sum[:, t : t + 1],
                 in1=exp_sb[:, t, :],
                 op0=ALU.mult,
                 op1=ALU.mult,
-                accum_out=shift[:, t : t + 1],
+                accum_out=dot[:, t : t + 1],
             )
 
         def centre(t):
+            nc.scalar.activation(
+                out=shift[:, t : t + 1], in_=dot[:, t : t + 1], func=ACT.Copy, scale=inv_sq[:, t : t + 1]
+            )
             nc.scalar.activation(
                 out=centred[t][:],
                 in_=d_ps[t][:, C:N_MOVING],
@@ -181,9 +189,20 @@ def tile_interfusion_pb_s_kernel(tc, logits1, logits2, x1, x2, grad_out, out):
             )
 
         def product(t):
-            engine = nc.gpsimd if t // C_TILES == 0 else nc.vector
-            engine.tensor_tensor(out=result[t][:], in0=centred[t][:], in1=exp_sb[:, t, :], op=ALU.mult)
-            nc.sync.dma_start(out=out_rows[t * P : (t + 1) * P, :], in_=result[t][:])
+            nc.gpsimd.tensor_tensor(out=result[t][:], in0=centred[t][:], in1=exp_sb[:, t, :], op=ALU.mult)
+
+        def store(t, queue):
+            queue.dma_start(out=out_rows[t * P : (t + 1) * P, :], in_=result[t][:])
+
+        def centre_and_product(t):
+            nc.vector.scalar_tensor_tensor(
+                out=result[t][:],
+                in0=d_ps[t][:, C:N_MOVING],
+                scalar=dot[:, t : t + 1],
+                in1=prob_sb[:, t - C_TILES, :],
+                op0=ALU.subtract,
+                op1=ALU.mult,
+            )
 
         load_g(0)
         load_x(0)
@@ -203,47 +222,54 @@ def tile_interfusion_pb_s_kernel(tc, logits1, logits2, x1, x2, grad_out, out):
 
         regroup_g(0, 0, "vector")
         regroup_g(0, 1, "scalar")
-        quantise_g(0, 0)
-        quantise_g(0, 1)
         transpose_x(0)
         copy_out_x(0)
-        nc.vector.reduce_max(out=row_max[:], in_=logit_sb[:], axis=AXIS.X)
-        nc.vector.tensor_scalar_mul(out=neg_max[:], in0=row_max[:], scalar1=-1.0)
+        quantise_g(0)
+        nc.vector.tensor_reduce(out=neg_max[:], in_=logit_sb[:], axis=AXIS.X, op=ALU.max, negate=True)
         transpose_x(1)
         regroup_g(1, 0, "vector")
         regroup_g(1, 1, "scalar")
         copy_out_x(1)
-        quantise_g(1, 0)
-        quantise_g(1, 1)
+        quantise_g(1)
         transpose_x(2)
         regroup_g(2, 0, "vector")
         regroup_g(2, 1, "scalar")
         quantise_x(0)
         copy_out_x(2)
-        quantise_g(2, 0)
         softmax_exp(0)
         transpose_x(3)
         regroup_g(3, 0, "vector")
         regroup_g(3, 1, "vector")
-        quantise_g(3, 0)
-        quantise_g(3, 1)
-        copy_out_x(3)
-        quantise_g(2, 1)
-        quantise_x(1)
-        for s in range(PASSES):
-            for ct in range(C_TILES):
+        for ct in range(C_TILES):
+            for s in range(PASSES):
                 multiply(s, ct)
+        quantise_g(2)
+        copy_out_x(3)
+        quantise_g(3)
         softmax_exp(1)
-        softmax_exp(2)
-        softmax_exp(3)
+        quantise_x(1)
         for ct in range(C_TILES):
             for s in range(PASSES, PIECES):
                 multiply(s, ct)
+        softmax_exp(2)
+        softmax_exp(3)
 
-        for b in range(B):
-            softmax_inverse(b)
-            for t in range(b * C_TILES, (b + 1) * C_TILES):
-                weighted_sum(t)
-            for t in range(b * C_TILES, (b + 1) * C_TILES):
-                centre(t)
-                product(t)
+        softmax_inverse(0)
+        weighted_sum(0)
+        softmax_inverse_squared()
+        softmax_inverse(1)
+        weighted_sum(1)
+        centre(0)
+        product(0)
+        probabilities(2)
+        centre(1)
+        product(1)
+        probabilities(3)
+        store(0, nc.scalar)
+        store(1, nc.scalar)
+        weighted_sum(2)
+        weighted_sum(3)
+        centre_and_product(2)
+        store(2, nc.sync)
+        centre_and_product(3)
+        store(3, nc.sync)

@@ -35,10 +35,10 @@ FLOPS = 2 * B * C * C * N_POS
 def tile_interfusion_pb_s_kernel(tc, logits1, logits2, x1, x2, grad_out, out):
     nc = tc.nc
 
-    logit_rows = logits1.flatten_outer_dims().rearrange("(t p) k -> p t k", p=P)
+    logit_rows = logits1.rearrange("b (p h) k -> p b (h k)", h=C_TILES)
     x_rows = x1.rearrange("b k h w -> (b k) (h w)")
     g_rows = grad_out.rearrange("b a h w -> (b a) (h w)")
-    out_rows = out.flatten_outer_dims()
+    out_tiles = out.rearrange("b (p h) k -> b h p k", h=C_TILES)
 
     with ExitStack() as ctx:
         keep = ctx.enter_context(tc.tile_pool(name="keep", bufs=1))
@@ -137,7 +137,7 @@ def tile_interfusion_pb_s_kernel(tc, logits1, logits2, x1, x2, grad_out, out):
         def regroup_g(s, ct, engine):
             cols = slice(ct * P, (ct + 1) * P)
             dst = g_grouped[s][:, cols, :].rearrange("p (c i) j -> p c j i", i=RUN)
-            src = g_raw[s][:, :, cols].rearrange("p j (c i) -> p c j i", i=RUN)
+            src = g_raw[s][:].rearrange("p j (c i h) -> p h c j i", i=RUN, h=C_TILES)[:, ct]
             if engine == "vector":
                 nc.vector.tensor_copy(out=dst, in_=src)
             else:
@@ -192,7 +192,7 @@ def tile_interfusion_pb_s_kernel(tc, logits1, logits2, x1, x2, grad_out, out):
             nc.gpsimd.tensor_tensor(out=result[t][:], in0=centred[t][:], in1=exp_sb[:, t, :], op=ALU.mult)
 
         def store(t, queue):
-            queue.dma_start(out=out_rows[t * P : (t + 1) * P, :], in_=result[t][:])
+            queue.dma_start(out=out_tiles[t // C_TILES, t % C_TILES], in_=result[t][:])
 
         def centre_and_product(t):
             nc.vector.scalar_tensor_tensor(
@@ -206,7 +206,7 @@ def tile_interfusion_pb_s_kernel(tc, logits1, logits2, x1, x2, grad_out, out):
 
         load_g(0)
         load_x(0)
-        nc.sync.dma_start(out=logit_sb[:], in_=logit_rows)
+        nc.sync.dma_start(out=logit_sb[:].rearrange("p (b h) k -> p b (h k)", b=B), in_=logit_rows)
         load_x(1)
         load_g(1)
         load_x(2)
@@ -236,7 +236,6 @@ def tile_interfusion_pb_s_kernel(tc, logits1, logits2, x1, x2, grad_out, out):
         regroup_g(2, 1, "scalar")
         quantise_x(0)
         copy_out_x(2)
-        softmax_exp(0)
         transpose_x(3)
         regroup_g(3, 0, "vector")
         regroup_g(3, 1, "vector")
@@ -246,6 +245,7 @@ def tile_interfusion_pb_s_kernel(tc, logits1, logits2, x1, x2, grad_out, out):
         quantise_g(2)
         copy_out_x(3)
         quantise_g(3)
+        softmax_exp(0)
         softmax_exp(1)
         quantise_x(1)
         for ct in range(C_TILES):

@@ -265,11 +265,11 @@ def tile_interfusion_pb_s_kernel(tc, logits1, logits2, x1, x2, grad_out, out):
         centre(1)
         product(1)
         probabilities(3)
-        store(0, nc.scalar)
-        store(1, nc.scalar)
         weighted_sum(2)
         weighted_sum(3)
         centre_and_product(2)
-        store(2, nc.sync)
         centre_and_product(3)
+        store(0, nc.sync)
+        store(2, nc.sync)
+        store(1, nc.sync)
         store(3, nc.sync)

@@ -55,7 +55,7 @@ def tile_interfusion_pb_s_kernel(tc, logits1, logits2, x1, x2, grad_out, out):
         exp_sb = keep.tile([P, ROW_TILES, C], F32)
         row_sum = keep.tile([P, ROW_TILES], F32)
         inv_sum = keep.tile([P, ROW_TILES], F32)
-        inv_sq = keep.tile([P, C_TILES], F32)
+        neg_inv_sq = keep.tile([P, C_TILES], F32)
         prob_sb = keep.tile([P, C_TILES, C], F32)
         x_grouped = keep.tile([P, B * PASSES * C * PACK], BF16, align_bytes=64)
         x_grouped_words = x_grouped[:].bitcast(F32).rearrange(
@@ -73,7 +73,6 @@ def tile_interfusion_pb_s_kernel(tc, logits1, logits2, x1, x2, grad_out, out):
         d_ps = [psum.tile([P, N_MOVING], F32, name="d_ps%d" % t) for t in range(ROW_TILES)]
         unread = [keep.tile([P, C], F32, name="unread%d" % t) for t in range(ROW_TILES)]
         dot = keep.tile([P, ROW_TILES], F32)
-        shift = keep.tile([P, C_TILES], F32)
         centred = [keep.tile([P, C], F32, name="centred%d" % t) for t in range(ROW_TILES)]
         result = [keep.tile([P, C], F32, name="result%d" % t) for t in range(ROW_TILES)]
 
@@ -122,8 +121,13 @@ def tile_interfusion_pb_s_kernel(tc, logits1, logits2, x1, x2, grad_out, out):
             nc.vector.reciprocal(out=inv_sum[:, tiles], in_=row_sum[:, tiles])
 
         def softmax_inverse_squared():
-            nc.vector.tensor_tensor(
-                out=inv_sq[:], in0=inv_sum[:, 0:C_TILES], in1=inv_sum[:, 0:C_TILES], op=ALU.mult
+            nc.vector.scalar_tensor_tensor(
+                out=neg_inv_sq[:],
+                in0=inv_sum[:, 0:C_TILES],
+                scalar=-1.0,
+                in1=inv_sum[:, 0:C_TILES],
+                op0=ALU.mult,
+                op1=ALU.mult,
             )
 
         def probabilities(t):
@@ -169,7 +173,7 @@ def tile_interfusion_pb_s_kernel(tc, logits1, logits2, x1, x2, grad_out, out):
             nc.vector.scalar_tensor_tensor(
                 out=unread[t][:],
                 in0=d_ps[t][:, C:N_MOVING],
-                scalar=-1.0 if t < C_TILES else inv_sum[:, t : t + 1],
+                scalar=neg_inv_sq[:, t : t + 1] if t < C_TILES else inv_sum[:, t : t + 1],
                 in1=exp_sb[:, t, :],
                 op0=ALU.mult,
                 op1=ALU.mult,
@@ -178,13 +182,10 @@ def tile_interfusion_pb_s_kernel(tc, logits1, logits2, x1, x2, grad_out, out):
 
         def centre(t):
             nc.scalar.activation(
-                out=shift[:, t : t + 1], in_=dot[:, t : t + 1], func=ACT.Copy, scale=inv_sq[:, t : t + 1]
-            )
-            nc.scalar.activation(
                 out=centred[t][:],
                 in_=d_ps[t][:, C:N_MOVING],
                 func=ACT.Identity,
-                bias=shift[:, t : t + 1],
+                bias=dot[:, t : t + 1],
                 scale=inv_sum[:, t : t + 1],
             )
 
@@ -236,6 +237,8 @@ def tile_interfusion_pb_s_kernel(tc, logits1, logits2, x1, x2, grad_out, out):
         regroup_g(2, 1, "scalar")
         quantise_x(0)
         copy_out_x(2)
+        softmax_exp(0)
+        softmax_exp(1)
         transpose_x(3)
         regroup_g(3, 0, "vector")
         regroup_g(3, 1, "vector")
@@ -244,9 +247,9 @@ def tile_interfusion_pb_s_kernel(tc, logits1, logits2, x1, x2, grad_out, out):
                 multiply(s, ct)
         quantise_g(2)
         copy_out_x(3)
+        softmax_inverse(0)
         quantise_g(3)
-        softmax_exp(0)
-        softmax_exp(1)
+        softmax_inverse_squared()
         quantise_x(1)
         for ct in range(C_TILES):
             for s in range(PASSES, PIECES):
@@ -254,11 +257,9 @@ def tile_interfusion_pb_s_kernel(tc, logits1, logits2, x1, x2, grad_out, out):
         softmax_exp(2)
         softmax_exp(3)
 
-        softmax_inverse(0)
         weighted_sum(0)
-        softmax_inverse_squared()
-        softmax_inverse(1)
         weighted_sum(1)
+        softmax_inverse(1)
         centre(0)
         product(0)
         probabilities(2)
@@ -271,5 +272,5 @@ def tile_interfusion_pb_s_kernel(tc, logits1, logits2, x1, x2, grad_out, out):
         centre_and_product(3)
         store(0, nc.sync)
         store(2, nc.sync)
-        store(1, nc.sync)
         store(3, nc.sync)
+        store(1, nc.sync)

@@ -229,27 +229,27 @@ def tile_interfusion_pb_s_kernel(tc, logits1, logits2, x1, x2, grad_out, out):
         nc.vector.tensor_reduce(out=neg_max[:], in_=logit_sb[:], axis=AXIS.X, op=ALU.max, negate=True)
         transpose_x(1)
         regroup_g(1, 0, "vector")
-        regroup_g(1, 1, "scalar")
+        regroup_g(1, 1, "vector")
         copy_out_x(1)
+        softmax_exp(0)
+        softmax_exp(1)
         quantise_g(1)
         transpose_x(2)
         regroup_g(2, 0, "vector")
         regroup_g(2, 1, "scalar")
         quantise_x(0)
+        softmax_inverse(0)
         copy_out_x(2)
-        softmax_exp(0)
-        softmax_exp(1)
         transpose_x(3)
         regroup_g(3, 0, "vector")
+        softmax_inverse_squared()
         regroup_g(3, 1, "vector")
         for ct in range(C_TILES):
             for s in range(PASSES):
                 multiply(s, ct)
         quantise_g(2)
         copy_out_x(3)
-        softmax_inverse(0)
         quantise_g(3)
-        softmax_inverse_squared()
         quantise_x(1)
         for ct in range(C_TILES):
             for s in range(PASSES, PIECES):

from contextlib import ExitStack

import concourse.masks as masks
import concourse.mybir as mybir

F32 = mybir.dt.float32
BF16 = mybir.dt.bfloat16
I32 = mybir.dt.int32
U32 = mybir.dt.uint32
U8 = mybir.dt.uint8
E4M3_X4 = mybir.dt.float8_e4m3fn_x4
E5M2_X4 = mybir.dt.float8_e5m2_x4
ALU = mybir.AluOpType
ACT = mybir.ActivationFunctionType
AXIS = mybir.AxisListType

B = 2
C = 256
N_POS = 1024
P = 128
PACK = 4
K_PASS = P * PACK
PASSES = N_POS // K_PASS
C_TILES = C // P
ROW_TILES = B * C_TILES
PAIR = 2
HALVES = PACK // PAIR
RUN = 4
PIECES = B * PASSES
N_MOVING = 2 * C

FLOPS = 2 * B * C * C * N_POS


def tile_interfusion_pb_s_kernel(tc, logits1, logits2, x1, x2, grad_out, out):
    nc = tc.nc

    logit_rows = logits1.rearrange("b (p h) k -> p b (h k)", h=C_TILES)
    x_rows = x1.rearrange("b k h w -> (b k) (h w)")
    g_rows = grad_out.rearrange("b a h w -> (b a) (h w)")
    out_tiles = out.rearrange("b (p h) k -> b h p k", h=C_TILES)

    with ExitStack() as ctx:
        keep = ctx.enter_context(tc.tile_pool(name="keep", bufs=1))
        psum = ctx.enter_context(tc.psum_pool(name="psum", bufs=1))
        ctx.enter_context(tc.manual_schedule())

        logit_sb = keep.tile([P, ROW_TILES, C], BF16)
        x_sb = [keep.tile([P, N_POS], BF16, name="x_sb%d" % r) for r in range(ROW_TILES)]
        g_raw = [keep.tile([P, PACK, C], BF16, name="g_raw%d" % s) for s in range(PIECES)]
        ident = keep.tile([P, P], F32)
        warm_in = keep.tile([P, 1], F32)
        warm_out = keep.tile([P, 1], F32)
        neg_max = keep.tile([P, ROW_TILES], F32)
        exp_sb = keep.tile([P, ROW_TILES, C], F32)
        row_sum = keep.tile([P, ROW_TILES], F32)
        inv_sum = keep.tile([P, ROW_TILES], F32)
        neg_inv_sq = keep.tile([P, C_TILES], F32)
        prob_sb = keep.tile([P, C_TILES, C], F32)
        x_grouped = keep.tile([P, B * PASSES * C * PACK], BF16, align_bytes=64)
        x_grouped_words = x_grouped[:].bitcast(F32).rearrange(
            "p (b g c u) -> p b g c u", b=B, g=PASSES, u=HALVES
        )
        x_codes = keep.tile([P, (1 + B * PASSES) * C], U32, align_bytes=64)
        x_scales = keep.tile([P, (1 + B * PASSES) * C], U8, align_bytes=64)
        x_t = [psum.tile([P, PASSES, HALVES, P], F32, name="x_t%d" % r) for r in range(ROW_TILES)]
        g_grouped = [
            keep.tile([P, C, PACK], BF16, name="g_grouped%d" % s, align_bytes=64)
            for s in range(PIECES)
        ]
        g_codes = [keep.tile([P, C], U32, name="g_codes%d" % s, align_bytes=64) for s in range(PIECES)]
        g_scales = [keep.tile([P, C], U8, name="g_scales%d" % s, align_bytes=64) for s in range(PIECES)]
        d_ps = [psum.tile([P, N_MOVING], F32, name="d_ps%d" % t) for t in range(ROW_TILES)]
        unread = [keep.tile([P, C], F32, name="unread%d" % t) for t in range(ROW_TILES)]
        dot = keep.tile([P, ROW_TILES], F32)
        centred = [keep.tile([P, C], F32, name="centred%d" % t) for t in range(ROW_TILES)]
        result = [keep.tile([P, C], F32, name="result%d" % t) for t in range(ROW_TILES)]

        def load_x(r):
            nc.sync.dma_start(out=x_sb[r][:], in_=x_rows[r * P : (r + 1) * P, :])

        def load_g(s):
            nc.sync.dma_start(
                out=g_raw[s][:].rearrange("p j c -> p (j c)"), in_=g_rows[s * P : (s + 1) * P, :]
            )

        def transpose_x(r):
            x_words = x_sb[r][:].bitcast(F32).rearrange("p (g i u) -> p g u i", g=PASSES, u=HALVES)
            for g in range(PASSES):
                for u in range(HALVES):
                    nc.tensor.transpose(x_t[r][:, g, u, :], x_words[:, g, u, :], ident[:])

        def copy_out_x(r):
            b = r // C_TILES
            h = r % C_TILES
            dst = x_grouped_words[:, b, :, h * P : (h + 1) * P, :]
            src = x_t[r][:].rearrange("p g u c -> p g c u")
            nc.scalar.copy(out=dst, in_=src)

        def quantise_x(b):
            first = (1 + b * PASSES) * C
            width = PASSES * C
            nc.vector.quantize_mx(
                out=x_codes[:, first : first + width].bitcast(E4M3_X4),
                scales=x_scales[:, first : first + width],
                in_=x_grouped[:, b * width * PACK : (b + 1) * width * PACK],
            )

        def softmax_exp(t):
            nc.scalar.activation(
                out=exp_sb[:, t, :],
                in_=logit_sb[:, t, :],
                func=ACT.Exp,
                bias=neg_max[:, t : t + 1],
                scale=1.0,
                accum_out=row_sum[:, t : t + 1],
            )

        def softmax_inverse(b):
            tiles = slice(b * C_TILES, (b + 1) * C_TILES)
            nc.vector.reciprocal(out=inv_sum[:, tiles], in_=row_sum[:, tiles])

        def softmax_inverse_squared():
            nc.vector.scalar_tensor_tensor(
                out=neg_inv_sq[:],
                in0=inv_sum[:, 0:C_TILES],
                scalar=-1.0,
                in1=inv_sum[:, 0:C_TILES],
                op0=ALU.mult,
                op1=ALU.mult,
            )

        def probabilities(t):
            nc.scalar.activation(
                out=prob_sb[:, t - C_TILES, :],
                in_=exp_sb[:, t, :],
                func=ACT.Copy,
                scale=inv_sum[:, t : t + 1],
            )

        def regroup_g(s, ct, engine):
            cols = slice(ct * P, (ct + 1) * P)
            dst = g_grouped[s][:, cols, :].rearrange("p (c i) j -> p c j i", i=RUN)
            src = g_raw[s][:].rearrange("p j (c i h) -> p h c j i", i=RUN, h=C_TILES)[:, ct]
            if engine == "vector":
                nc.vector.tensor_copy(out=dst, in_=src)
            else:
                nc.scalar.copy(out=dst, in_=src)

        def quantise_g(s):
            nc.vector.quantize_mx(
                out=g_codes[s][:].bitcast(E5M2_X4),
                scales=g_scales[s][:],
                in_=g_grouped[s][:].rearrange("p c j -> p (c j)"),
            )

        def multiply(s, ct):
            b = s // PASSES
            g = s % PASSES
            cols = slice(ct * P, (ct + 1) * P)
            first = (b * PASSES + g) * C
            nc.tensor.matmul_mx(
                out=d_ps[b * C_TILES + ct][:],
                lhsT=g_codes[s][:, cols].bitcast(E5M2_X4),
                lhsT_scale=g_scales[s][:, cols],
                rhs=x_codes[:, first : first + N_MOVING].bitcast(E4M3_X4),
                rhs_scale=x_scales[:, first : first + N_MOVING],
                start=(g == 0),
                stop=(g == PASSES - 1),
            )

        def weighted_sum(t):
            nc.vector.scalar_tensor_tensor(
                out=unread[t][:],
                in0=d_ps[t][:, C:N_MOVING],
                scalar=neg_inv_sq[:, t : t + 1] if t < C_TILES else inv_sum[:, t : t + 1],
                in1=exp_sb[:, t, :],
                op0=ALU.mult,
                op1=ALU.mult,
                accum_out=dot[:, t : t + 1],
            )

        def centre(t):
            nc.scalar.activation(
                out=centred[t][:],
                in_=d_ps[t][:, C:N_MOVING],
                func=ACT.Identity,
                bias=dot[:, t : t + 1],
                scale=inv_sum[:, t : t + 1],
            )

        def product(t):
            nc.gpsimd.tensor_tensor(out=result[t][:], in0=centred[t][:], in1=exp_sb[:, t, :], op=ALU.mult)

        def store(t, queue):
            queue.dma_start(out=out_tiles[t // C_TILES, t % C_TILES], in_=result[t][:])

        def centre_and_product(t):
            nc.vector.scalar_tensor_tensor(
                out=result[t][:],
                in0=d_ps[t][:, C:N_MOVING],
                scalar=dot[:, t : t + 1],
                in1=prob_sb[:, t - C_TILES, :],
                op0=ALU.subtract,
                op1=ALU.mult,
            )

        load_g(0)
        load_x(0)
        nc.sync.dma_start(out=logit_sb[:].rearrange("p (b h) k -> p b (h k)", b=B), in_=logit_rows)
        load_x(1)
        load_g(1)
        load_x(2)
        load_g(2)
        load_x(3)
        load_g(3)

        masks.make_identity(nc, ident[:])
        nc.vector.memset(warm_in[:], 0.0)
        nc.scalar.activation(out=warm_out[:], in_=warm_in[:], func=ACT.Exp)
        nc.vector.memset(x_codes[:, 0:C].bitcast(I32), 0)
        nc.vector.memset(x_scales[:, 0:C].bitcast(I32), 0)

        regroup_g(0, 0, "vector")
        regroup_g(0, 1, "scalar")
        transpose_x(0)
        copy_out_x(0)
        quantise_g(0)
        nc.vector.tensor_reduce(out=neg_max[:], in_=logit_sb[:], axis=AXIS.X, op=ALU.max, negate=True)
        transpose_x(1)
        regroup_g(1, 0, "vector")
        regroup_g(1, 1, "vector")
        copy_out_x(1)
        softmax_exp(0)
        softmax_exp(1)
        quantise_g(1)
        transpose_x(2)
        regroup_g(2, 0, "vector")
        regroup_g(2, 1, "scalar")
        quantise_x(0)
        softmax_inverse(0)
        copy_out_x(2)
        transpose_x(3)
        regroup_g(3, 0, "vector")
        softmax_inverse_squared()
        regroup_g(3, 1, "vector")
        for ct in range(C_TILES):
            for s in range(PASSES):
                multiply(s, ct)
        quantise_g(2)
        copy_out_x(3)
        quantise_g(3)
        quantise_x(1)
        for ct in range(C_TILES):
            for s in range(PASSES, PIECES):
                multiply(s, ct)
        softmax_exp(2)
        softmax_exp(3)

        weighted_sum(0)
        weighted_sum(1)
        softmax_inverse(1)
        centre(0)
        product(0)
        probabilities(2)
        centre(1)
        product(1)
        probabilities(3)
        weighted_sum(2)
        weighted_sum(3)
        centre_and_product(2)
        centre_and_product(3)
        store(0, nc.sync)
        store(2, nc.sync)
        store(3, nc.sync)
        store(1, nc.sync)
